import numpy as np
import ml_dtypes


def mxq(x, axis, fmt="e4m3"):
    dtype, down = {"e4m3": (ml_dtypes.float8_e4m3fn, 7), "e5m2": (ml_dtypes.float8_e5m2, 14)}[fmt]
    v = np.moveaxis(np.asarray(x, np.float32).astype(ml_dtypes.bfloat16).astype(np.float64), axis, -1)
    blocks = v.reshape(v.shape[:-1] + (-1, 32))
    amax = np.abs(blocks).max(-1, keepdims=True)
    byte = np.maximum(np.where(amax > 0, np.frexp(amax)[1] - 1 + 127, 0) - down, 1)
    scale = np.exp2(byte - 127.0)
    codes = (blocks / scale).astype(np.float32).astype(dtype).astype(np.float64)
    return np.moveaxis((codes * scale).reshape(v.shape), -1, axis)


WIDE = False


def mx_kscale(k):
    if not WIDE:
        return np.ones(k)
    levels = np.array([30, -30])
    if k % 512:
        return np.exp2(np.random.permutation(np.resize(levels, k // 32))).repeat(32)
    a = np.empty((k // 512, 16))
    for p in range(k // 512):
        a[p, :8] = np.random.permutation(np.resize(levels, 8))
        for g in range(8):
            far = levels[np.abs(levels - a[p, g]) >= 10]
            a[p, g + 8] = far[np.random.randint(len(far))]
    return np.exp2(a.ravel()).repeat(32)


BF16 = ml_dtypes.bfloat16


def bf(x):
    return np.asarray(x, np.float32).astype(BF16)


def f64(x):
    return np.asarray(x).astype(np.float64)


B, S, I0, I1, I2, N0, N1, N2 = 4, 256, 512, 1024, 2048, 512, 512, 1024


def blk(fan_in, width, s):
    return bf(np.random.uniform(-1.0, 1.0, (fan_in, width)) / np.sqrt(fan_in) / s[:fan_in, None])


def setup_inputs():
    s = mx_kscale(I2)
    return {"x": bf(np.random.standard_normal((B, S, I2)) * s),
            "w0": blk(I0, N0, s), "w1": blk(I1, N1, s), "w2": blk(I2, N2, s),
            "bias": bf(np.random.standard_normal(N0 + N1 + N2) * 0.1)}


def reference(x, w0, w1, w2, bias):
    xq = mxq(f64(x), 2, "e5m2")
    y0 = xq[:, :, :I0] @ mxq(f64(w0), 0, "e4m3")
    y1 = xq[:, :, :I1] @ mxq(f64(w1), 0, "e4m3")
    y2 = xq @ mxq(f64(w2), 0, "e4m3")
    return np.concatenate([y0, y1, y2], axis=2) + f64(bias)

@@ -1,0 +1,266 @@
+from contextlib import ExitStack
+
+import concourse.mybir as mybir
+from concourse.masks import make_identity
+
+F32 = mybir.dt.float32
+BF16 = mybir.dt.bfloat16
+I32 = mybir.dt.int32
+U32 = mybir.dt.uint32
+U8 = mybir.dt.uint8
+E4M3X4 = mybir.dt.float8_e4m3fn_x4
+E5M2X4 = mybir.dt.float8_e5m2_x4
+
+P = 128
+PACK = 4
+K_PASS = P * PACK
+N_TILE = 512
+TOKENS, FEATURES, COLUMNS = 1024, 2048, 2048
+TILES = TOKENS // P
+HALF = FEATURES // 2
+BANKS = 8
+FLOPS = 2 * TOKENS * (512 * 512 + 1024 * 512 + 2048 * 1024)
+
+EARLY = 3
+OPEN = 4
+SINGLES = 4
+
+BLOCKS = {"y0": (0, 1), "y1": (512, 2), "y2l": (1024, 4), "y2r": (1536, 4)}
+
+
+def tile_mlinear_kernel(tc, x, w0, w1, w2, bias, out):
+    nc = tc.nc
+    x_rows = x.flatten_outer_dims().rearrange("(p j) k -> p j k", j=TILES)
+    out_rows = out.flatten_outer_dims().rearrange("(p j) c -> p (j c)", j=TILES)
+    weights = {"y0": w0, "y1": w1, "y2l": w2[:, :N_TILE], "y2r": w2[:, N_TILE:]}
+
+    with ExitStack() as ctx:
+        keep = ctx.enter_context(tc.tile_pool(name="keep", bufs=1))
+        stage = ctx.enter_context(tc.tile_pool(name="stage", bufs=4))
+        psum = ctx.enter_context(tc.psum_pool(name="psum", bufs=1))
+        ctx.enter_context(tc.manual_schedule())
+
+        free_banks = list(range(BANKS))
+        x_raw, x_grouped, x_codes, x_scales = {}, {}, {}, {}
+        w_raw, w_grouped, w_codes, w_scales = {}, {}, {}, {}
+        sums = {}
+        staged = {}
+
+        def load_x(tiles, halves):
+            name = "x_raw%d_%d" % (tiles[0], halves[0])
+            cols = slice(halves[0] * HALF, (halves[-1] + 1) * HALF)
+            raw = keep.tile([P, len(tiles), len(halves) * HALF], BF16, name=name)
+            nc.sync.dma_start(out=raw[:], in_=x_rows[:, tiles[0] : tiles[-1] + 1, cols])
+            for a, j in enumerate(tiles):
+                for b, h in enumerate(halves):
+                    x_raw[j, h] = raw[:, a, b * HALF : (b + 1) * HALF]
+
+        def load_w(block, g):
+            raw = keep.tile([P, PACK, N_TILE], BF16, name="w_raw_%s%d" % (block, g))
+            rows = weights[block][g * K_PASS : (g + 1) * K_PASS, :]
+            nc.sync.dma_start(out=raw[:], in_=rows.rearrange("(p t) n -> p t n", t=PACK))
+            w_raw[block, g] = raw
+
+        def turn_x(j, h):
+            bank = free_banks.pop(0)
+            turned = psum.tile([P, 2, 2, P], F32, name="turned", tag="bank%d" % bank)
+            words = x_raw[j, h].bitcast(F32)
+            for g in range(2):
+                for u in range(2):
+                    nc.tensor.transpose(turned[:, g, u, :], words[:, 2 * P * g + u : 2 * P * (g + 1) : 2], ident[:])
+            grouped = stage.tile([P, HALF], BF16, name="x_grouped", align_bytes=64)
+            nc.scalar.copy(
+                out=grouped[:].bitcast(F32).rearrange("p (g r u) -> p g r u", g=2, u=2),
+                in_=turned[:].rearrange("p g u r -> p g r u"),
+            )
+            x_grouped[j, h] = grouped
+            free_banks.append(bank)
+
+        def quantize_x(j, h):
+            codes = keep.tile([P, 2 * P], U32, name="x_codes%d_%d" % (j, h), align_bytes=64)
+            scales = keep.tile([P, 2 * P], U8, name="x_scales%d_%d" % (j, h), align_bytes=64)
+            nc.vector.quantize_mx(out=codes[:].bitcast(E5M2X4), scales=scales[:], in_=x_grouped[j, h][:])
+            x_codes[j, h], x_scales[j, h] = codes, scales
+
+        def group_w(block, g, copy, first, last):
+            if (block, g) not in w_grouped:
+                grouped = stage.tile([P, N_TILE * PACK], BF16, name="w_grouped", align_bytes=64)
+                w_grouped[block, g] = grouped
+            copy(
+                out=w_grouped[block, g][:, first * PACK : last * PACK].rearrange("p (c i t) -> p c t i", i=4, t=PACK),
+                in_=w_raw[block, g][:, :, first:last].rearrange("p t (c i) -> p c t i", i=4),
+            )
+
+        def group_w_vector(block, g, first=0, last=N_TILE):
+            group_w(block, g, nc.vector.tensor_copy, first, last)
+
+        def group_w_scalar(block, g, first=0, last=N_TILE):
+            group_w(block, g, nc.scalar.copy, first, last)
+
+        def quantize_w(block, g):
+            codes = keep.tile([P, N_TILE], U32, name="w_codes_%s%d" % (block, g), align_bytes=64)
+            scales = keep.tile([P, N_TILE], U8, name="w_scales_%s%d" % (block, g), align_bytes=64)
+            nc.vector.quantize_mx(out=codes[:].bitcast(E4M3X4), scales=scales[:], in_=w_grouped[block, g][:])
+            w_codes[block, g], w_scales[block, g] = codes, scales
+
+        def multiply(j, block, passes):
+            for g in passes:
+                if g == 0:
+                    bank = free_banks.pop(0)
+                    acc = psum.tile([P, N_TILE], F32, name="acc", tag="bank%d" % bank)
+                    sums[j, block] = (acc, bank)
+                tokens = slice((g % 2) * P, (g % 2 + 1) * P)
+                nc.tensor.matmul_mx(
+                    out=sums[j, block][0][:],
+                    lhsT=x_codes[j, g // 2][:, tokens].bitcast(E5M2X4),
+                    lhsT_scale=x_scales[j, g // 2][:, tokens],
+                    rhs=w_codes[block, g][:].bitcast(E4M3X4),
+                    rhs_scale=w_scales[block, g][:],
+                    start=(g == 0),
+                    stop=(g == BLOCKS[block][1] - 1),
+                )
+
+        def finish(j, block):
+            acc, bank = sums[j, block]
+            column = BLOCKS[block][0]
+            at = j * COLUMNS + column
+            pair = (at + N_TILE) // (2 * N_TILE)
+            first = max(pair * 2 * N_TILE - N_TILE, 0)
+            last = min(pair * 2 * N_TILE + N_TILE, TILES * COLUMNS)
+            if pair not in staged:
+                result = keep.tile([P, last - first], F32, name="result%d" % pair)
+                staged[pair] = [result, 0]
+            result = staged[pair][0]
+            nc.vector.tensor_tensor(
+                out=result[:, at - first : at - first + N_TILE],
+                in0=acc[:],
+                in1=bias_rows[:, column : column + N_TILE],
+                op=mybir.AluOpType.add,
+            )
+            free_banks.append(bank)
+            staged[pair][1] += N_TILE
+            if pair % 2 == 1 and j < SINGLES:
+                nc.sync.dma_start(out=out_rows[:, at : at + N_TILE], in_=result[:, at - first : at - first + N_TILE])
+            elif staged[pair][1] == last - first:
+                nc.sync.dma_start(out=out_rows[:, first:last], in_=result[:])
+
+        ident = keep.tile([P, P], F32, name="ident")
+        make_identity(nc, ident[:])
+        bias_row0 = keep.tile([P, COLUMNS], BF16, name="bias_row0")
+        nc.vector.memset(bias_row0[:].bitcast(I32), 0)
+        nc.scalar.dma_start(out=bias_row0[0:1, :], in_=bias.unsqueeze(0))
+        pick_row0 = keep.tile([P, P], BF16, name="pick_row0")
+        nc.scalar.copy(out=pick_row0[:], in_=ident[:, 0:1].to_broadcast([P, P]))
+        bias_rows = keep.tile([P, COLUMNS], BF16, name="bias_rows")
+
+        def spread_bias():
+            for first in range(0, COLUMNS, 2 * N_TILE):
+                bank = free_banks.pop(0)
+                spread = psum.tile([P, 2 * N_TILE], BF16, name="spread", tag="bank%d" % bank)
+                for c in range(0, 2 * N_TILE, N_TILE):
+                    nc.tensor.matmul(
+                        out=spread[:, c : c + N_TILE],
+                        lhsT=pick_row0[:],
+                        rhs=bias_row0[:, first + c : first + c + N_TILE],
+                        start=True,
+                        stop=True,
+                    )
+                nc.scalar.copy(out=bias_rows[:, first : first + 2 * N_TILE], in_=spread[:])
+                free_banks.append(bank)
+
+        load_x([0], [0])
+        load_w("y1", 0)
+        load_x([0], [1])
+        load_x([1], [0, 1])
+        load_w("y1", 1)
+        for g in range(3):
+            load_x([2 * g + 2], [0, 1])
+            load_x([2 * g + 3], [0, 1])
+            load_w("y2l", g)
+        later = [("y2r", 0), ("y2r", 1), ("y0", 0), ("y2r", 2), ("y2r", 3)]
+        for block, g in [("y2l", 3)] + later:
+            load_w(block, g)
+
+        mid = N_TILE // 2
+
+        turn_x(0, 0)
+        group_w_vector("y1", 0)
+        spread_bias()
+        quantize_x(0, 0)
+        quantize_w("y1", 0)
+        turn_x(0, 1)
+        turn_x(1, 0)
+        multiply(0, "y1", [0])
+        turn_x(1, 1)
+        group_w_vector("y1", 1)
+        quantize_x(1, 0)
+        quantize_x(0, 1)
+        quantize_w("y1", 1)
+        quantize_x(1, 1)
+        multiply(1, "y1", [0])
+
+        for g in range(3):
+            a, b = 2 * g + 2, 2 * g + 3
+            turn_x(a, 0)
+            turn_x(a, 1)
+            if g == 0:
+                multiply(0, "y1", [1])
+                multiply(1, "y1", [1])
+            else:
+                multiply(a - 1, "y1", [0, 1])
+            quantize_x(a, 0)
+            if g > 0:
+                finish(a - 3, "y1")
+                quantize_w("y2l", g - 1)
+            quantize_x(a, 1)
+            turn_x(b, 0)
+            turn_x(b, 1)
+            multiply(a, "y1", [0, 1])
+            if g > 0:
+                for j in range(EARLY):
+                    multiply(j, "y2l", [g - 1])
+            finish(a - 2, "y1")
+            quantize_x(b, 0)
+            group_w_vector("y2l", g, 0, mid)
+            group_w_scalar("y2l", g, mid)
+            quantize_x(b, 1)
+
+        multiply(7, "y1", [0, 1])
+        finish(5, "y1")
+        group_w_vector("y2l", 3, 0, mid)
+        group_w_scalar("y2l", 3, mid)
+        quantize_w("y2l", 2)
+        multiply(EARLY, "y2l", [0, 1])
+        finish(6, "y1")
+        quantize_w("y2l", 3)
+        multiply(EARLY + 1, "y2l", [0, 1])
+        group_w_vector("y2r", 0, 0, mid)
+        group_w_scalar("y2r", 0, mid)
+        finish(7, "y1")
+        for j in range(EARLY + 2):
+            multiply(j, "y2l", [2])
+        for j in range(TILES):
+            if j % 2 == 0:
+                group_w_scalar(*later[j // 2 + 1])
+            multiply(j, "y2l", [3] if j < EARLY + 2 else range(4))
+            finish(j, "y2l")
+            if j % 2 == 1:
+                quantize_w(*later[j // 2])
+
+        for j in range(OPEN):
+            multiply(j, "y2r", [0, 1])
+        for j in range(OPEN):
+            multiply(j, "y0", [0])
+            finish(j, "y0")
+            if j == 1:
+                quantize_w(*later[-1])
+        for j in range(OPEN):
+            multiply(j, "y2r", [2])
+        for j in range(TILES):
+            if j < OPEN:
+                multiply(j, "y2r", [3])
+            else:
+                multiply(j, "y0", [0])
+                multiply(j, "y2r", range(4))
+                finish(j, "y0")
+            finish(j, "y2r")

@@ -21,9 +21,10 @@ HALF = FEATURES // 2
 BANKS = 8
 FLOPS = 2 * TOKENS * (512 * 512 + 1024 * 512 + 2048 * 1024)
 
-EARLY = 3
+TURN_BANKS = 3
+EARLY = 4
 OPEN = 4
-SINGLES = 4
+SINGLES = 2
 
 BLOCKS = {"y0": (0, 1), "y1": (512, 2), "y2l": (1024, 4), "y2r": (1536, 4)}
 
@@ -40,7 +41,8 @@ def tile_mlinear_kernel(tc, x, w0, w1, w2, bias, out):
         psum = ctx.enter_context(tc.psum_pool(name="psum", bufs=1))
         ctx.enter_context(tc.manual_schedule())
 
-        free_banks = list(range(BANKS))
+        turn_banks = list(range(TURN_BANKS))
+        free_banks = list(range(TURN_BANKS, BANKS))
         x_raw, x_grouped, x_codes, x_scales = {}, {}, {}, {}
         w_raw, w_grouped, w_codes, w_scales = {}, {}, {}, {}
         sums = {}
@@ -62,7 +64,7 @@ def tile_mlinear_kernel(tc, x, w0, w1, w2, bias, out):
             w_raw[block, g] = raw
 
         def turn_x(j, h):
-            bank = free_banks.pop(0)
+            bank = turn_banks.pop(0)
             turned = psum.tile([P, 2, 2, P], F32, name="turned", tag="bank%d" % bank)
             words = x_raw[j, h].bitcast(F32)
             for g in range(2):
@@ -74,7 +76,7 @@ def tile_mlinear_kernel(tc, x, w0, w1, w2, bias, out):
                 in_=turned[:].rearrange("p g u r -> p g r u"),
             )
             x_grouped[j, h] = grouped
-            free_banks.append(bank)
+            turn_banks.append(bank)
 
         def quantize_x(j, h):
             codes = keep.tile([P, 2 * P], U32, name="x_codes%d_%d" % (j, h), align_bytes=64)
@@ -148,28 +150,33 @@ def tile_mlinear_kernel(tc, x, w0, w1, w2, bias, out):
         make_identity(nc, ident[:])
         bias_row0 = keep.tile([P, COLUMNS], BF16, name="bias_row0")
         nc.vector.memset(bias_row0[:].bitcast(I32), 0)
-        nc.scalar.dma_start(out=bias_row0[0:1, :], in_=bias.unsqueeze(0))
         pick_row0 = keep.tile([P, P], BF16, name="pick_row0")
         nc.scalar.copy(out=pick_row0[:], in_=ident[:, 0:1].to_broadcast([P, P]))
         bias_rows = keep.tile([P, COLUMNS], BF16, name="bias_rows")
 
-        def spread_bias():
-            for first in range(0, COLUMNS, 2 * N_TILE):
-                bank = free_banks.pop(0)
-                spread = psum.tile([P, 2 * N_TILE], BF16, name="spread", tag="bank%d" % bank)
-                for c in range(0, 2 * N_TILE, N_TILE):
-                    nc.tensor.matmul(
-                        out=spread[:, c : c + N_TILE],
-                        lhsT=pick_row0[:],
-                        rhs=bias_row0[:, first + c : first + c + N_TILE],
-                        start=True,
-                        stop=True,
-                    )
-                nc.scalar.copy(out=bias_rows[:, first : first + 2 * N_TILE], in_=spread[:])
-                free_banks.append(bank)
+        spread = {}
+
+        def spread_bias(half):
+            bank = free_banks.pop(0)
+            rows = psum.tile([P, HALF], BF16, name="spread", tag="bank%d" % bank)
+            for c in range(0, HALF, N_TILE):
+                nc.tensor.matmul(
+                    out=rows[:, c : c + N_TILE],
+                    lhsT=pick_row0[:],
+                    rhs=bias_row0[:, half * HALF + c : half * HALF + c + N_TILE],
+                    start=True,
+                    stop=True,
+                )
+            spread[half] = (rows, bank)
+
+        def keep_bias(half):
+            rows, bank = spread[half]
+            nc.scalar.copy(out=bias_rows[:, half * HALF : (half + 1) * HALF], in_=rows[:])
+            free_banks.append(bank)
 
         load_x([0], [0])
         load_w("y1", 0)
+        nc.sync.dma_start(out=bias_row0[0:1, :], in_=bias.unsqueeze(0))
         load_x([0], [1])
         load_x([1], [0, 1])
         load_w("y1", 1)
@@ -184,75 +191,80 @@ def tile_mlinear_kernel(tc, x, w0, w1, w2, bias, out):
         mid = N_TILE // 2
 
         turn_x(0, 0)
-        group_w_vector("y1", 0)
-        spread_bias()
+        group_w_vector("y1", 0, 0, mid)
         quantize_x(0, 0)
-        quantize_w("y1", 0)
+        group_w_vector("y1", 0, mid)
+        spread_bias(0)
         turn_x(0, 1)
         turn_x(1, 0)
-        multiply(0, "y1", [0])
         turn_x(1, 1)
-        group_w_vector("y1", 1)
-        quantize_x(1, 0)
+        quantize_w("y1", 0)
+        multiply(0, "y1", [0])
         quantize_x(0, 1)
-        quantize_w("y1", 1)
-        quantize_x(1, 1)
+        quantize_x(1, 0)
         multiply(1, "y1", [0])
+        spread_bias(1)
+        keep_bias(0)
+        keep_bias(1)
+        group_w_vector("y1", 1)
+        quantize_x(1, 1)
+        quantize_w("y1", 1)
 
         for g in range(3):
             a, b = 2 * g + 2, 2 * g + 3
-            turn_x(a, 0)
-            turn_x(a, 1)
+            for j in (a, b):
+                turn_x(j, 0)
+                turn_x(j, 1)
+            group_w_scalar("y2l", g, mid)
+            quantize_x(a, 0)
             if g == 0:
                 multiply(0, "y1", [1])
-                multiply(1, "y1", [1])
             else:
-                multiply(a - 1, "y1", [0, 1])
-            quantize_x(a, 0)
-            if g > 0:
-                finish(a - 3, "y1")
-                quantize_w("y2l", g - 1)
+                finish(a - 2, "y1")
             quantize_x(a, 1)
-            turn_x(b, 0)
-            turn_x(b, 1)
-            multiply(a, "y1", [0, 1])
-            if g > 0:
-                for j in range(EARLY):
-                    multiply(j, "y2l", [g - 1])
-            finish(a - 2, "y1")
             quantize_x(b, 0)
             group_w_vector("y2l", g, 0, mid)
-            group_w_scalar("y2l", g, mid)
             quantize_x(b, 1)
+            multiply(a - 1, "y1", [0, 1] if g else [1])
+            multiply(a, "y1", [0, 1])
+            if g == 0:
+                finish(0, "y1")
+            if g == 1:
+                multiply(0, "y2l", [0])
+            if g < 2:
+                finish(a - 1, "y1")
+                quantize_w("y2l", g)
 
+        free_banks.extend(turn_banks)
         multiply(7, "y1", [0, 1])
-        finish(5, "y1")
         group_w_vector("y2l", 3, 0, mid)
         group_w_scalar("y2l", 3, mid)
         quantize_w("y2l", 2)
-        multiply(EARLY, "y2l", [0, 1])
-        finish(6, "y1")
+        finish(5, "y1")
         quantize_w("y2l", 3)
-        multiply(EARLY + 1, "y2l", [0, 1])
         group_w_vector("y2r", 0, 0, mid)
         group_w_scalar("y2r", 0, mid)
+        finish(6, "y1")
+        quantize_w("y2r", 0)
         finish(7, "y1")
-        for j in range(EARLY + 2):
+        for j in range(EARLY):
+            multiply(j, "y2l", [1] if j == 0 else [0, 1])
+        for j in range(EARLY):
             multiply(j, "y2l", [2])
         for j in range(TILES):
-            if j % 2 == 0:
-                group_w_scalar(*later[j // 2 + 1])
-            multiply(j, "y2l", [3] if j < EARLY + 2 else range(4))
+            if j % 3 == 0:
+                group_w_scalar(*later[j // 3 + 1])
+            multiply(j, "y2l", [3] if j < EARLY else range(4))
             finish(j, "y2l")
-            if j % 2 == 1:
-                quantize_w(*later[j // 2])
+            if j % 3 == 1:
+                quantize_w(*later[j // 3 + 1])
+        group_w_scalar(*later[-1])
 
         for j in range(OPEN):
             multiply(j, "y2r", [0, 1])
-        for j in range(OPEN):
             multiply(j, "y0", [0])
             finish(j, "y0")
-            if j == 1:
+            if j == 2:
                 quantize_w(*later[-1])
         for j in range(OPEN):
             multiply(j, "y2r", [2])

@@ -24,7 +24,17 @@ FLOPS = 2 * TOKENS * (512 * 512 + 1024 * 512 + 2048 * 1024)
 TURN_BANKS = 3
 EARLY = 4
 OPEN = 4
-SINGLES = 2
+SINGLES = 8
+WARM = 0
+A1S = 0
+B2V = 1
+SPLIT = 256
+JOINED = 0
+C1S = 1
+BV = 0
+LAG = 3
+QAT = 1
+WIDE = 1
 
 BLOCKS = {"y0": (0, 1), "y1": (512, 2), "y2l": (1024, 4), "y2r": (1536, 4)}
 
@@ -45,7 +55,7 @@ def tile_mlinear_kernel(tc, x, w0, w1, w2, bias, out):
         free_banks = list(range(TURN_BANKS, BANKS))
         x_raw, x_grouped, x_codes, x_scales = {}, {}, {}, {}
         w_raw, w_grouped, w_codes, w_scales = {}, {}, {}, {}
-        sums = {}
+        sums, passes_done = {}, {}
         staged = {}
 
         def load_x(tiles, halves):
@@ -63,6 +73,13 @@ def tile_mlinear_kernel(tc, x, w0, w1, w2, bias, out):
             nc.sync.dma_start(out=raw[:], in_=rows.rearrange("(p t) n -> p t n", t=PACK))
             w_raw[block, g] = raw
 
+        def load_w2(g):
+            raw = keep.tile([P, PACK, 2 * N_TILE], BF16, name="w_raw_w2%d" % g)
+            rows = w2[g * K_PASS : (g + 1) * K_PASS, :]
+            nc.sync.dma_start(out=raw[:], in_=rows.rearrange("(p t) n -> p t n", t=PACK))
+            w_raw["y2l", g] = raw[:, :, :N_TILE]
+            w_raw["y2r", g] = raw[:, :, N_TILE:]
+
         def turn_x(j, h):
             bank = turn_banks.pop(0)
             turned = psum.tile([P, 2, 2, P], F32, name="turned", tag="bank%d" % bank)
@@ -70,7 +87,7 @@ def tile_mlinear_kernel(tc, x, w0, w1, w2, bias, out):
             for g in range(2):
                 for u in range(2):
                     nc.tensor.transpose(turned[:, g, u, :], words[:, 2 * P * g + u : 2 * P * (g + 1) : 2], ident[:])
-            grouped = stage.tile([P, HALF], BF16, name="x_grouped", align_bytes=64)
+            grouped = stage.tile([P, HALF], BF16, name="x_grouped", bufs=6, align_bytes=64)
             nc.scalar.copy(
                 out=grouped[:].bitcast(F32).rearrange("p (g r u) -> p g r u", g=2, u=2),
                 in_=turned[:].rearrange("p g u r -> p g r u"),
@@ -107,10 +124,12 @@ def tile_mlinear_kernel(tc, x, w0, w1, w2, bias, out):
 
         def multiply(j, block, passes):
             for g in passes:
-                if g == 0:
+                if (j, block) not in sums:
                     bank = free_banks.pop(0)
                     acc = psum.tile([P, N_TILE], F32, name="acc", tag="bank%d" % bank)
                     sums[j, block] = (acc, bank)
+                done = passes_done.get((j, block), 0)
+                passes_done[j, block] = done + 1
                 tokens = slice((g % 2) * P, (g % 2 + 1) * P)
                 nc.tensor.matmul_mx(
                     out=sums[j, block][0][:],
@@ -118,8 +137,8 @@ def tile_mlinear_kernel(tc, x, w0, w1, w2, bias, out):
                     lhsT_scale=x_scales[j, g // 2][:, tokens],
                     rhs=w_codes[block, g][:].bitcast(E4M3X4),
                     rhs_scale=w_scales[block, g][:],
-                    start=(g == 0),
-                    stop=(g == BLOCKS[block][1] - 1),
+                    start=(done == 0),
+                    stop=(done == BLOCKS[block][1] - 1),
                 )
 
         def finish(j, block):
@@ -141,7 +160,7 @@ def tile_mlinear_kernel(tc, x, w0, w1, w2, bias, out):
             )
             free_banks.append(bank)
             staged[pair][1] += N_TILE
-            if pair % 2 == 1 and j < SINGLES:
+            if (j < SINGLES) if pair % 2 == 1 else (pair // 2 > JOINED):
                 nc.sync.dma_start(out=out_rows[:, at : at + N_TILE], in_=result[:, at - first : at - first + N_TILE])
             elif staged[pair][1] == last - first:
                 nc.sync.dma_start(out=out_rows[:, first:last], in_=result[:])
@@ -171,7 +190,7 @@ def tile_mlinear_kernel(tc, x, w0, w1, w2, bias, out):
 
         def keep_bias(half):
             rows, bank = spread[half]
-            nc.scalar.copy(out=bias_rows[:, half * HALF : (half + 1) * HALF], in_=rows[:])
+            (nc.vector.tensor_copy if BV else nc.scalar.copy)(out=bias_rows[:, half * HALF : (half + 1) * HALF], in_=rows[:])
             free_banks.append(bank)
 
         load_x([0], [0])
@@ -179,76 +198,120 @@ def tile_mlinear_kernel(tc, x, w0, w1, w2, bias, out):
         nc.sync.dma_start(out=bias_row0[0:1, :], in_=bias.unsqueeze(0))
         load_x([0], [1])
         load_x([1], [0, 1])
+        load_x([2], [0, 1])
         load_w("y1", 1)
-        for g in range(3):
-            load_x([2 * g + 2], [0, 1])
-            load_x([2 * g + 3], [0, 1])
+        load_x([3], [0, 1])
+        for g in range(2):
             load_w("y2l", g)
-        later = [("y2r", 0), ("y2r", 1), ("y0", 0), ("y2r", 2), ("y2r", 3)]
-        for block, g in [("y2l", 3)] + later:
-            load_w(block, g)
+            load_x([2 * g + 4], [0, 1])
+            load_x([2 * g + 5], [0, 1])
+        if not WIDE:
+            load_w("y2l", 2)
+        if WIDE:
+            load_w2(2)
+            load_w2(3)
+            later = [("y2r", 2), ("y2r", 3), ("y0", 0), ("y2r", 0), ("y2r", 1)]
+            for block, g in later[2:]:
+                load_w(block, g)
+            order = [2, 3, 0, 1]
+        else:
+            later = [("y2r", 0), ("y2r", 1), ("y0", 0), ("y2r", 2), ("y2r", 3)]
+            for block, g in [("y2l", 3)] + later:
+                load_w(block, g)
+            order = [0, 1, 2, 3]
 
         mid = N_TILE // 2
 
+        def turn_tile(j):
+            turn_x(j, 0)
+            turn_x(j, 1)
+
+        if WARM:
+            idle = keep.tile([P, N_TILE], BF16, name="idle")
+            nc.gpsimd.memset(idle[:].bitcast(I32), 0)
+            unread = psum.tile([P, N_TILE], F32, name="unread", tag="bank%d" % free_banks[-1])
+            for w in range(WARM):
+                nc.tensor.matmul(out=unread[:], lhsT=idle[:, :P], rhs=idle[:], start=True, stop=True)
         turn_x(0, 0)
-        group_w_vector("y1", 0, 0, mid)
-        quantize_x(0, 0)
-        group_w_vector("y1", 0, mid)
         spread_bias(0)
         turn_x(0, 1)
-        turn_x(1, 0)
-        turn_x(1, 1)
+        turn_tile(1)
+        group_w_vector("y1", 0)
+        quantize_x(0, 0)
         quantize_w("y1", 0)
-        multiply(0, "y1", [0])
         quantize_x(0, 1)
-        quantize_x(1, 0)
-        multiply(1, "y1", [0])
+        multiply(0, "y1", [0])
         spread_bias(1)
         keep_bias(0)
         keep_bias(1)
-        group_w_vector("y1", 1)
+        turn_tile(2)
+        quantize_x(1, 0)
         quantize_x(1, 1)
+        multiply(1, "y1", [0])
+        group_w_vector("y1", 1)
+        quantize_x(2, 0)
         quantize_w("y1", 1)
+        quantize_x(2, 1)
+        turn_tile(3)
+        group_w_scalar("y2l", 0, mid)
+        multiply(2, "y1", [0])
+        for j in range(3):
+            multiply(j, "y1", [1])
+        group_w_vector("y2l", 0, 0, mid)
+        quantize_x(3, 0)
+        finish(0, "y1")
+        multiply(3, "y1", [0, 1])
+        quantize_w("y2l", 0)
+        quantize_x(3, 1)
+        finish(1, "y1")
 
-        for g in range(3):
-            a, b = 2 * g + 2, 2 * g + 3
-            for j in (a, b):
-                turn_x(j, 0)
-                turn_x(j, 1)
-            group_w_scalar("y2l", g, mid)
-            quantize_x(a, 0)
-            if g == 0:
-                multiply(0, "y1", [1])
-            else:
-                finish(a - 2, "y1")
-            quantize_x(a, 1)
-            quantize_x(b, 0)
-            group_w_vector("y2l", g, 0, mid)
-            quantize_x(b, 1)
-            multiply(a - 1, "y1", [0, 1] if g else [1])
-            multiply(a, "y1", [0, 1])
-            if g == 0:
-                finish(0, "y1")
-            if g == 1:
-                multiply(0, "y2l", [0])
-            if g < 2:
-                finish(a - 1, "y1")
-                quantize_w("y2l", g)
+        turn_tile(4)
+        if A1S:
+            group_w_scalar("y2l", 1, 0, mid)
+        multiply(0, "y2l", [0])
+        multiply(1, "y2l", [0])
+        quantize_x(4, 0)
+        finish(2, "y1")
+        quantize_x(4, 1)
+        finish(3, "y1")
+        turn_tile(5)
+        group_w_scalar("y2l", 1, mid)
+        multiply(4, "y1", [0, 1])
+        quantize_x(5, 0)
+        if not A1S:
+            group_w_vector("y2l", 1, 0, mid)
+        finish(4, "y1")
+        quantize_x(5, 1)
+        turn_tile(6)
+        multiply(5, "y1", [0, 1])
+        quantize_w("y2l", 1)
+        quantize_x(6, 0)
+        group_w_vector("y2l", 2, 0, SPLIT)
+        quantize_x(6, 1)
+        finish(5, "y1")
+        turn_tile(7)
+        group_w_scalar("y2l", 2, SPLIT)
+        multiply(6, "y1", [0, 1])
+        multiply(0, "y2l", [1])
+        multiply(1, "y2l", [1])
+        quantize_x(7, 0)
+        group_w_vector("y2l", 3, 0, SPLIT)
+        quantize_x(7, 1)
 
         free_banks.extend(turn_banks)
         multiply(7, "y1", [0, 1])
-        group_w_vector("y2l", 3, 0, mid)
-        group_w_scalar("y2l", 3, mid)
         quantize_w("y2l", 2)
-        finish(5, "y1")
-        quantize_w("y2l", 3)
-        group_w_vector("y2r", 0, 0, mid)
-        group_w_scalar("y2r", 0, mid)
+        group_w_scalar("y2l", 3, SPLIT)
         finish(6, "y1")
-        quantize_w("y2r", 0)
+        quantize_w("y2l", 3)
         finish(7, "y1")
-        for j in range(EARLY):
-            multiply(j, "y2l", [1] if j == 0 else [0, 1])
+        if B2V:
+            group_w_vector(*later[0], 0, mid)
+            group_w_scalar(*later[0], mid)
+        else:
+            group_w_scalar(*later[0])
+        for j in range(2, EARLY):
+            multiply(j, "y2l", [0, 1])
         for j in range(EARLY):
             multiply(j, "y2l", [2])
         for j in range(TILES):
@@ -256,23 +319,21 @@ def tile_mlinear_kernel(tc, x, w0, w1, w2, bias, out):
                 group_w_scalar(*later[j // 3 + 1])
             multiply(j, "y2l", [3] if j < EARLY else range(4))
             finish(j, "y2l")
-            if j % 3 == 1:
+            if j == 0:
+                quantize_w(*later[0])
+            if j % 3 == QAT or (QAT == 2 and j == 7):
                 quantize_w(*later[j // 3 + 1])
         group_w_scalar(*later[-1])
 
         for j in range(OPEN):
-            multiply(j, "y2r", [0, 1])
-            multiply(j, "y0", [0])
-            finish(j, "y0")
-            if j == 2:
-                quantize_w(*later[-1])
+            multiply(j, "y2r", order[:2])
+            for i in range(j * TILES // OPEN, (j + 1) * TILES // OPEN):
+                multiply(i, "y0", [0])
+                finish(i, "y0")
+                if i == LAG:
+                    quantize_w(*later[-1])
         for j in range(OPEN):
-            multiply(j, "y2r", [2])
+            multiply(j, "y2r", order[2:3])
         for j in range(TILES):
-            if j < OPEN:
-                multiply(j, "y2r", [3])
-            else:
-                multiply(j, "y0", [0])
-                multiply(j, "y2r", range(4))
-                finish(j, "y0")
+            multiply(j, "y2r", order[3:] if j < OPEN else order)
             finish(j, "y2r")

@@ -32,17 +32,21 @@ SPLIT = 256
 JOINED = 0
 C1S = 1
 BV = 0
-LAG = 3
-QAT = 1
+LAG = 4
+QS = [0, 2, 5]
+LAG0 = 0
+M01 = 0
+MP = 1
 WIDE = 1
+STORE_TILES = {"y0": 1, "y1": 4, "y2l": 2, "y2r": 2}
 
 BLOCKS = {"y0": (0, 1), "y1": (512, 2), "y2l": (1024, 4), "y2r": (1536, 4)}
 
 
 def tile_mlinear_kernel(tc, x, w0, w1, w2, bias, out):
     nc = tc.nc
-    x_rows = x.flatten_outer_dims().rearrange("(p j) k -> p j k", j=TILES)
-    out_rows = out.flatten_outer_dims().rearrange("(p j) c -> p (j c)", j=TILES)
+    x_rows = x.flatten_outer_dims().rearrange("(p j) k -> p (j k)", j=TILES)
+    out_rows = out.flatten_outer_dims().rearrange("(p j) c -> p j c", j=TILES)
     weights = {"y0": w0, "y1": w1, "y2l": w2[:, :N_TILE], "y2r": w2[:, N_TILE:]}
 
     with ExitStack() as ctx:
@@ -58,14 +62,11 @@ def tile_mlinear_kernel(tc, x, w0, w1, w2, bias, out):
         sums, passes_done = {}, {}
         staged = {}
 
-        def load_x(tiles, halves):
-            name = "x_raw%d_%d" % (tiles[0], halves[0])
-            cols = slice(halves[0] * HALF, (halves[-1] + 1) * HALF)
-            raw = keep.tile([P, len(tiles), len(halves) * HALF], BF16, name=name)
-            nc.sync.dma_start(out=raw[:], in_=x_rows[:, tiles[0] : tiles[-1] + 1, cols])
-            for a, j in enumerate(tiles):
-                for b, h in enumerate(halves):
-                    x_raw[j, h] = raw[:, a, b * HALF : (b + 1) * HALF]
+        def load_x(first, count):
+            raw = keep.tile([P, count * HALF], BF16, name="x_raw%d" % first)
+            nc.sync.dma_start(out=raw[:], in_=x_rows[:, first * HALF : (first + count) * HALF])
+            for n in range(count):
+                x_raw[divmod(first + n, 2)] = raw[:, n * HALF : (n + 1) * HALF]
 
         def load_w(block, g):
             raw = keep.tile([P, PACK, N_TILE], BF16, name="w_raw_%s%d" % (block, g))
@@ -144,26 +145,20 @@ def tile_mlinear_kernel(tc, x, w0, w1, w2, bias, out):
         def finish(j, block):
             acc, bank = sums[j, block]
             column = BLOCKS[block][0]
-            at = j * COLUMNS + column
-            pair = (at + N_TILE) // (2 * N_TILE)
-            first = max(pair * 2 * N_TILE - N_TILE, 0)
-            last = min(pair * 2 * N_TILE + N_TILE, TILES * COLUMNS)
-            if pair not in staged:
-                result = keep.tile([P, last - first], F32, name="result%d" % pair)
-                staged[pair] = [result, 0]
-            result = staged[pair][0]
+            count = 1 if block == "y2r" and j >= OPEN else STORE_TILES[block]
+            first = j - j % count
+            if j == first:
+                result = keep.tile([P, count, N_TILE], F32, name="result_%s%d" % (block, j))
+                staged[block] = result
             nc.vector.tensor_tensor(
-                out=result[:, at - first : at - first + N_TILE],
+                out=staged[block][:, j - first, :],
                 in0=acc[:],
                 in1=bias_rows[:, column : column + N_TILE],
                 op=mybir.AluOpType.add,
             )
             free_banks.append(bank)
-            staged[pair][1] += N_TILE
-            if (j < SINGLES) if pair % 2 == 1 else (pair // 2 > JOINED):
-                nc.sync.dma_start(out=out_rows[:, at : at + N_TILE], in_=result[:, at - first : at - first + N_TILE])
-            elif staged[pair][1] == last - first:
-                nc.sync.dma_start(out=out_rows[:, first:last], in_=result[:])
+            if j == first + count - 1:
+                nc.sync.dma_start(out=out_rows[:, first : j + 1, column : column + N_TILE], in_=staged[block][:])
 
         ident = keep.tile([P, P], F32, name="ident")
         make_identity(nc, ident[:])
@@ -193,18 +188,24 @@ def tile_mlinear_kernel(tc, x, w0, w1, w2, bias, out):
             (nc.vector.tensor_copy if BV else nc.scalar.copy)(out=bias_rows[:, half * HALF : (half + 1) * HALF], in_=rows[:])
             free_banks.append(bank)
 
-        load_x([0], [0])
+        load_x(0, 1)
         load_w("y1", 0)
         nc.sync.dma_start(out=bias_row0[0:1, :], in_=bias.unsqueeze(0))
-        load_x([0], [1])
-        load_x([1], [0, 1])
-        load_x([2], [0, 1])
+        if M01:
+            load_x(1, 3)
+        else:
+            load_x(1, 1)
+            load_x(2, 2)
+        load_x(4, 2)
         load_w("y1", 1)
-        load_x([3], [0, 1])
+        load_x(6, 2)
         for g in range(2):
             load_w("y2l", g)
-            load_x([2 * g + 4], [0, 1])
-            load_x([2 * g + 5], [0, 1])
+            if MP:
+                load_x(4 * g + 8, 4)
+            else:
+                load_x(4 * g + 8, 2)
+                load_x(4 * g + 10, 2)
         if not WIDE:
             load_w("y2l", 2)
         if WIDE:
@@ -266,34 +267,35 @@ def tile_mlinear_kernel(tc, x, w0, w1, w2, bias, out):
         finish(1, "y1")
 
         turn_tile(4)
-        if A1S:
-            group_w_scalar("y2l", 1, 0, mid)
+        turn_tile(5)
+        group_w_scalar("y2l", 1, 0 if A1S else mid)
         multiply(0, "y2l", [0])
         multiply(1, "y2l", [0])
         quantize_x(4, 0)
         finish(2, "y1")
         quantize_x(4, 1)
         finish(3, "y1")
-        turn_tile(5)
-        group_w_scalar("y2l", 1, mid)
         multiply(4, "y1", [0, 1])
         quantize_x(5, 0)
         if not A1S:
             group_w_vector("y2l", 1, 0, mid)
-        finish(4, "y1")
         quantize_x(5, 1)
-        turn_tile(6)
+        if A1S:
+            for j in range(2, EARLY):
+                multiply(j, "y2l", [0])
         multiply(5, "y1", [0, 1])
+        finish(4, "y1")
+        turn_tile(6)
+        turn_tile(7)
         quantize_w("y2l", 1)
         quantize_x(6, 0)
         group_w_vector("y2l", 2, 0, SPLIT)
         quantize_x(6, 1)
         finish(5, "y1")
-        turn_tile(7)
         group_w_scalar("y2l", 2, SPLIT)
-        multiply(6, "y1", [0, 1])
         multiply(0, "y2l", [1])
         multiply(1, "y2l", [1])
+        multiply(6, "y1", [0, 1])
         quantize_x(7, 0)
         group_w_vector("y2l", 3, 0, SPLIT)
         quantize_x(7, 1)
@@ -311,25 +313,26 @@ def tile_mlinear_kernel(tc, x, w0, w1, w2, bias, out):
         else:
             group_w_scalar(*later[0])
         for j in range(2, EARLY):
-            multiply(j, "y2l", [0, 1])
+            multiply(j, "y2l", [1] if A1S else [0, 1])
         for j in range(EARLY):
             multiply(j, "y2l", [2])
         for j in range(TILES):
-            if j % 3 == 0:
-                group_w_scalar(*later[j // 3 + 1])
             multiply(j, "y2l", [3] if j < EARLY else range(4))
             finish(j, "y2l")
             if j == 0:
-                quantize_w(*later[0])
-            if j % 3 == QAT or (QAT == 2 and j == 7):
-                quantize_w(*later[j // 3 + 1])
-        group_w_scalar(*later[-1])
+                group_w_scalar(*later[1])
+            if j in QS:
+                n = QS.index(j)
+                quantize_w(*later[n])
+                group_w_scalar(*later[n + 2])
 
         for j in range(OPEN):
             multiply(j, "y2r", order[:2])
             for i in range(j * TILES // OPEN, (j + 1) * TILES // OPEN):
                 multiply(i, "y0", [0])
                 finish(i, "y0")
+                if i == LAG0:
+                    quantize_w(*later[-2])
                 if i == LAG:
                     quantize_w(*later[-1])
         for j in range(OPEN):

@@ -107,8 +107,8 @@ def tile_mlinear_kernel(tc, x, w0, w1, w2, bias, out):
                 grouped = stage.tile([P, N_TILE * PACK], BF16, name="w_grouped", align_bytes=64)
                 w_grouped[block, g] = grouped
             copy(
-                out=w_grouped[block, g][:, first * PACK : last * PACK].rearrange("p (c i t) -> p c t i", i=4, t=PACK),
-                in_=w_raw[block, g][:, :, first:last].rearrange("p t (c i) -> p c t i", i=4),
+                out=w_grouped[block, g][:, first * PACK : last * PACK].rearrange("p (n t) -> p n t", t=PACK),
+                in_=w_raw[block, g][:, :, first:last].rearrange("p t n -> p n t"),
             )
 
         def group_w_vector(block, g, first=0, last=N_TILE):

from contextlib import ExitStack

import concourse.mybir as mybir
from concourse.masks import make_identity

F32 = mybir.dt.float32
BF16 = mybir.dt.bfloat16
I32 = mybir.dt.int32
U32 = mybir.dt.uint32
U8 = mybir.dt.uint8
E4M3X4 = mybir.dt.float8_e4m3fn_x4
E5M2X4 = mybir.dt.float8_e5m2_x4

P = 128
PACK = 4
K_PASS = P * PACK
N_TILE = 512
TOKENS, FEATURES, COLUMNS = 1024, 2048, 2048
TILES = TOKENS // P
HALF = FEATURES // 2
BANKS = 8
FLOPS = 2 * TOKENS * (512 * 512 + 1024 * 512 + 2048 * 1024)

TURN_BANKS = 3
EARLY = 4
OPEN = 4
SINGLES = 8
WARM = 0
A1S = 0
B2V = 1
SPLIT = 256
JOINED = 0
C1S = 1
BV = 0
LAG = 4
QS = [0, 2, 5]
LAG0 = 0
M01 = 0
MP = 1
WIDE = 1
STORE_TILES = {"y0": 1, "y1": 4, "y2l": 2, "y2r": 2}

BLOCKS = {"y0": (0, 1), "y1": (512, 2), "y2l": (1024, 4), "y2r": (1536, 4)}


def tile_mlinear_kernel(tc, x, w0, w1, w2, bias, out):
    nc = tc.nc
    x_rows = x.flatten_outer_dims().rearrange("(p j) k -> p (j k)", j=TILES)
    out_rows = out.flatten_outer_dims().rearrange("(p j) c -> p j c", j=TILES)
    weights = {"y0": w0, "y1": w1, "y2l": w2[:, :N_TILE], "y2r": w2[:, N_TILE:]}

    with ExitStack() as ctx:
        keep = ctx.enter_context(tc.tile_pool(name="keep", bufs=1))
        stage = ctx.enter_context(tc.tile_pool(name="stage", bufs=4))
        psum = ctx.enter_context(tc.psum_pool(name="psum", bufs=1))
        ctx.enter_context(tc.manual_schedule())

        turn_banks = list(range(TURN_BANKS))
        free_banks = list(range(TURN_BANKS, BANKS))
        x_raw, x_grouped, x_codes, x_scales = {}, {}, {}, {}
        w_raw, w_grouped, w_codes, w_scales = {}, {}, {}, {}
        sums, passes_done = {}, {}
        staged = {}

        def load_x(first, count):
            raw = keep.tile([P, count * HALF], BF16, name="x_raw%d" % first)
            nc.sync.dma_start(out=raw[:], in_=x_rows[:, first * HALF : (first + count) * HALF])
            for n in range(count):
                x_raw[divmod(first + n, 2)] = raw[:, n * HALF : (n + 1) * HALF]

        def load_w(block, g):
            raw = keep.tile([P, PACK, N_TILE], BF16, name="w_raw_%s%d" % (block, g))
            rows = weights[block][g * K_PASS : (g + 1) * K_PASS, :]
            nc.sync.dma_start(out=raw[:], in_=rows.rearrange("(p t) n -> p t n", t=PACK))
            w_raw[block, g] = raw

        def load_w2(g):
            raw = keep.tile([P, PACK, 2 * N_TILE], BF16, name="w_raw_w2%d" % g)
            rows = w2[g * K_PASS : (g + 1) * K_PASS, :]
            nc.sync.dma_start(out=raw[:], in_=rows.rearrange("(p t) n -> p t n", t=PACK))
            w_raw["y2l", g] = raw[:, :, :N_TILE]
            w_raw["y2r", g] = raw[:, :, N_TILE:]

        def turn_x(j, h):
            bank = turn_banks.pop(0)
            turned = psum.tile([P, 2, 2, P], F32, name="turned", tag="bank%d" % bank)
            words = x_raw[j, h].bitcast(F32)
            for g in range(2):
                for u in range(2):
                    nc.tensor.transpose(turned[:, g, u, :], words[:, 2 * P * g + u : 2 * P * (g + 1) : 2], ident[:])
            grouped = stage.tile([P, HALF], BF16, name="x_grouped", bufs=6, align_bytes=64)
            nc.scalar.copy(
                out=grouped[:].bitcast(F32).rearrange("p (g r u) -> p g r u", g=2, u=2),
                in_=turned[:].rearrange("p g u r -> p g r u"),
            )
            x_grouped[j, h] = grouped
            turn_banks.append(bank)

        def quantize_x(j, h):
            codes = keep.tile([P, 2 * P], U32, name="x_codes%d_%d" % (j, h), align_bytes=64)
            scales = keep.tile([P, 2 * P], U8, name="x_scales%d_%d" % (j, h), align_bytes=64)
            nc.vector.quantize_mx(out=codes[:].bitcast(E5M2X4), scales=scales[:], in_=x_grouped[j, h][:])
            x_codes[j, h], x_scales[j, h] = codes, scales

        def group_w(block, g, copy, first, last):
            if (block, g) not in w_grouped:
                grouped = stage.tile([P, N_TILE * PACK], BF16, name="w_grouped", align_bytes=64)
                w_grouped[block, g] = grouped
            copy(
                out=w_grouped[block, g][:, first * PACK : last * PACK].rearrange("p (n t) -> p n t", t=PACK),
                in_=w_raw[block, g][:, :, first:last].rearrange("p t n -> p n t"),
            )

        def group_w_vector(block, g, first=0, last=N_TILE):
            group_w(block, g, nc.vector.tensor_copy, first, last)

        def group_w_scalar(block, g, first=0, last=N_TILE):
            group_w(block, g, nc.scalar.copy, first, last)

        def quantize_w(block, g):
            codes = keep.tile([P, N_TILE], U32, name="w_codes_%s%d" % (block, g), align_bytes=64)
            scales = keep.tile([P, N_TILE], U8, name="w_scales_%s%d" % (block, g), align_bytes=64)
            nc.vector.quantize_mx(out=codes[:].bitcast(E4M3X4), scales=scales[:], in_=w_grouped[block, g][:])
            w_codes[block, g], w_scales[block, g] = codes, scales

        def multiply(j, block, passes):
            for g in passes:
                if (j, block) not in sums:
                    bank = free_banks.pop(0)
                    acc = psum.tile([P, N_TILE], F32, name="acc", tag="bank%d" % bank)
                    sums[j, block] = (acc, bank)
                done = passes_done.get((j, block), 0)
                passes_done[j, block] = done + 1
                tokens = slice((g % 2) * P, (g % 2 + 1) * P)
                nc.tensor.matmul_mx(
                    out=sums[j, block][0][:],
                    lhsT=x_codes[j, g // 2][:, tokens].bitcast(E5M2X4),
                    lhsT_scale=x_scales[j, g // 2][:, tokens],
                    rhs=w_codes[block, g][:].bitcast(E4M3X4),
                    rhs_scale=w_scales[block, g][:],
                    start=(done == 0),
                    stop=(done == BLOCKS[block][1] - 1),
                )

        def finish(j, block):
            acc, bank = sums[j, block]
            column = BLOCKS[block][0]
            count = 1 if block == "y2r" and j >= OPEN else STORE_TILES[block]
            first = j - j % count
            if j == first:
                result = keep.tile([P, count, N_TILE], F32, name="result_%s%d" % (block, j))
                staged[block] = result
            nc.vector.tensor_tensor(
                out=staged[block][:, j - first, :],
                in0=acc[:],
                in1=bias_rows[:, column : column + N_TILE],
                op=mybir.AluOpType.add,
            )
            free_banks.append(bank)
            if j == first + count - 1:
                nc.sync.dma_start(out=out_rows[:, first : j + 1, column : column + N_TILE], in_=staged[block][:])

        ident = keep.tile([P, P], F32, name="ident")
        make_identity(nc, ident[:])
        bias_row0 = keep.tile([P, COLUMNS], BF16, name="bias_row0")
        nc.vector.memset(bias_row0[:].bitcast(I32), 0)
        pick_row0 = keep.tile([P, P], BF16, name="pick_row0")
        nc.scalar.copy(out=pick_row0[:], in_=ident[:, 0:1].to_broadcast([P, P]))
        bias_rows = keep.tile([P, COLUMNS], BF16, name="bias_rows")

        spread = {}

        def spread_bias(half):
            bank = free_banks.pop(0)
            rows = psum.tile([P, HALF], BF16, name="spread", tag="bank%d" % bank)
            for c in range(0, HALF, N_TILE):
                nc.tensor.matmul(
                    out=rows[:, c : c + N_TILE],
                    lhsT=pick_row0[:],
                    rhs=bias_row0[:, half * HALF + c : half * HALF + c + N_TILE],
                    start=True,
                    stop=True,
                )
            spread[half] = (rows, bank)

        def keep_bias(half):
            rows, bank = spread[half]
            (nc.vector.tensor_copy if BV else nc.scalar.copy)(out=bias_rows[:, half * HALF : (half + 1) * HALF], in_=rows[:])
            free_banks.append(bank)

        load_x(0, 1)
        load_w("y1", 0)
        nc.sync.dma_start(out=bias_row0[0:1, :], in_=bias.unsqueeze(0))
        if M01:
            load_x(1, 3)
        else:
            load_x(1, 1)
            load_x(2, 2)
        load_x(4, 2)
        load_w("y1", 1)
        load_x(6, 2)
        for g in range(2):
            load_w("y2l", g)
            if MP:
                load_x(4 * g + 8, 4)
            else:
                load_x(4 * g + 8, 2)
                load_x(4 * g + 10, 2)
        if not WIDE:
            load_w("y2l", 2)
        if WIDE:
            load_w2(2)
            load_w2(3)
            later = [("y2r", 2), ("y2r", 3), ("y0", 0), ("y2r", 0), ("y2r", 1)]
            for block, g in later[2:]:
                load_w(block, g)
            order = [2, 3, 0, 1]
        else:
            later = [("y2r", 0), ("y2r", 1), ("y0", 0), ("y2r", 2), ("y2r", 3)]
            for block, g in [("y2l", 3)] + later:
                load_w(block, g)
            order = [0, 1, 2, 3]

        mid = N_TILE // 2

        def turn_tile(j):
            turn_x(j, 0)
            turn_x(j, 1)

        if WARM:
            idle = keep.tile([P, N_TILE], BF16, name="idle")
            nc.gpsimd.memset(idle[:].bitcast(I32), 0)
            unread = psum.tile([P, N_TILE], F32, name="unread", tag="bank%d" % free_banks[-1])
            for w in range(WARM):
                nc.tensor.matmul(out=unread[:], lhsT=idle[:, :P], rhs=idle[:], start=True, stop=True)
        turn_x(0, 0)
        spread_bias(0)
        turn_x(0, 1)
        turn_tile(1)
        group_w_vector("y1", 0)
        quantize_x(0, 0)
        quantize_w("y1", 0)
        quantize_x(0, 1)
        multiply(0, "y1", [0])
        spread_bias(1)
        keep_bias(0)
        keep_bias(1)
        turn_tile(2)
        quantize_x(1, 0)
        quantize_x(1, 1)
        multiply(1, "y1", [0])
        group_w_vector("y1", 1)
        quantize_x(2, 0)
        quantize_w("y1", 1)
        quantize_x(2, 1)
        turn_tile(3)
        group_w_scalar("y2l", 0, mid)
        multiply(2, "y1", [0])
        for j in range(3):
            multiply(j, "y1", [1])
        group_w_vector("y2l", 0, 0, mid)
        quantize_x(3, 0)
        finish(0, "y1")
        multiply(3, "y1", [0, 1])
        quantize_w("y2l", 0)
        quantize_x(3, 1)
        finish(1, "y1")

        turn_tile(4)
        turn_tile(5)
        group_w_scalar("y2l", 1, 0 if A1S else mid)
        multiply(0, "y2l", [0])
        multiply(1, "y2l", [0])
        quantize_x(4, 0)
        finish(2, "y1")
        quantize_x(4, 1)
        finish(3, "y1")
        multiply(4, "y1", [0, 1])
        quantize_x(5, 0)
        if not A1S:
            group_w_vector("y2l", 1, 0, mid)
        quantize_x(5, 1)
        if A1S:
            for j in range(2, EARLY):
                multiply(j, "y2l", [0])
        multiply(5, "y1", [0, 1])
        finish(4, "y1")
        turn_tile(6)
        turn_tile(7)
        quantize_w("y2l", 1)
        quantize_x(6, 0)
        group_w_vector("y2l", 2, 0, SPLIT)
        quantize_x(6, 1)
        finish(5, "y1")
        group_w_scalar("y2l", 2, SPLIT)
        multiply(0, "y2l", [1])
        multiply(1, "y2l", [1])
        multiply(6, "y1", [0, 1])
        quantize_x(7, 0)
        group_w_vector("y2l", 3, 0, SPLIT)
        quantize_x(7, 1)

        free_banks.extend(turn_banks)
        multiply(7, "y1", [0, 1])
        quantize_w("y2l", 2)
        group_w_scalar("y2l", 3, SPLIT)
        finish(6, "y1")
        quantize_w("y2l", 3)
        finish(7, "y1")
        if B2V:
            group_w_vector(*later[0], 0, mid)
            group_w_scalar(*later[0], mid)
        else:
            group_w_scalar(*later[0])
        for j in range(2, EARLY):
            multiply(j, "y2l", [1] if A1S else [0, 1])
        for j in range(EARLY):
            multiply(j, "y2l", [2])
        for j in range(TILES):
            multiply(j, "y2l", [3] if j < EARLY else range(4))
            finish(j, "y2l")
            if j == 0:
                group_w_scalar(*later[1])
            if j in QS:
                n = QS.index(j)
                quantize_w(*later[n])
                group_w_scalar(*later[n + 2])

        for j in range(OPEN):
            multiply(j, "y2r", order[:2])
            for i in range(j * TILES // OPEN, (j + 1) * TILES // OPEN):
                multiply(i, "y0", [0])
                finish(i, "y0")
                if i == LAG0:
                    quantize_w(*later[-2])
                if i == LAG:
                    quantize_w(*later[-1])
        for j in range(OPEN):
            multiply(j, "y2r", order[2:3])
        for j in range(TILES):
            multiply(j, "y2r", order[3:] if j < OPEN else order)
            finish(j, "y2r")
